import numpy as np
import ml_dtypes

BF16 = ml_dtypes.bfloat16


def bf(x):
    return np.asarray(x, np.float32).astype(BF16)


def f32(x):
    return np.asarray(x, np.float32)


def f64(x):
    return np.asarray(x).astype(np.float64)


def striped(idx):
    return np.tile(idx.reshape(-1, 16).T, (8, 1))


S, D, T, M, N = 1024, 128, 128, 256, 512


def setup_inputs():
    e = np.arange(T)
    freq = np.exp(-(e - e % 2) * (np.log(10000.0) / T))
    phase = (e % 2) * (np.pi / 2.0)
    return {"table": bf(np.random.standard_normal((D, S))), "w": bf(np.random.standard_normal((D, M)) / np.sqrt(D + T)), "wt": bf(np.random.standard_normal((T, M)) / np.sqrt(D + T)), "b": f32(0.1 * np.random.standard_normal((M, 1))), "t": f32(np.sort(1.5 * np.random.random_sample((1, N)), axis=-1)), "freq": f32(freq.reshape(T, 1)), "phase": f32(phase.reshape(T, 1)), "offs": striped(np.random.permutation(np.tile(np.arange(S), 2))[:N])}


def reference(table, w, wt, b, t, freq, phase, offs):
    idx = offs[:16].T.reshape(-1)
    tem = np.sin(f64(freq) * f64(t) + f64(phase))
    return f64(w).T @ f64(table)[:, idx] + f64(wt).T @ tem + f64(b)

@@ -1,0 +1,60 @@
+import concourse.mybir as mybir
+
+BF16, F32, U16 = mybir.dt.bfloat16, mybir.dt.float32, mybir.dt.uint16
+SIN = mybir.ActivationFunctionType.Sin
+IDENTITY = mybir.ActivationFunctionType.Identity
+
+P = 128
+S = 1024
+N = 512
+HALVES = 2
+
+FLOPS = 2 * (P + P) * (HALVES * P) * N
+
+
+def tile_xfmrnhpfast_kernel(tc, table, w, wt, b, t, freq, phase, offs, out):
+    nc = tc.nc
+    with (
+        tc.tile_pool(name="held", bufs=1) as held,
+        tc.psum_pool(name="psum", bufs=1) as psum,
+    ):
+        offsets = held.tile([P, N // 16], U16, name="offsets")
+        nc.sync.dma_start(offsets[:], offs)
+        window = held.tile([P, S], BF16, name="window")
+        nc.sync.dma_start(window[:], table)
+        w_sb = held.tile([P, HALVES * P], BF16, name="w_sb")
+        nc.sync.dma_start(w_sb[:], w)
+
+        t_all = held.tile([P, N], F32, name="t_all")
+        nc.scalar.dma_start(t_all[:], t.to_broadcast([P, N]))
+        freq_sb = held.tile([P, 1], F32, name="freq_sb")
+        nc.scalar.dma_start(freq_sb[:], freq)
+        phase_sb = held.tile([P, 1], F32, name="phase_sb")
+        nc.scalar.dma_start(phase_sb[:], phase)
+
+        wt_sb = held.tile([P, HALVES * P], BF16, name="wt_sb")
+        nc.gpsimd.dma_start(wt_sb[:], wt)
+        bias = [held.tile([P, 1], F32, name=f"bias{h}") for h in range(HALVES)]
+        for h in range(HALVES):
+            nc.gpsimd.dma_start(bias[h][:], b[h * P : (h + 1) * P, :])
+
+        tem = held.tile([P, N], BF16, name="tem")
+        nc.scalar.activation(tem[:], t_all[:], SIN, bias=phase_sb[:], scale=freq_sb[:])
+
+        banks = [psum.tile([P, N], F32, name=f"bank{h}") for h in range(HALVES)]
+        for h in range(HALVES):
+            nc.tensor.matmul(
+                banks[h][:],
+                w_sb[:, h * P : (h + 1) * P],
+                window[:].indirect(offsets[:]),
+                start=True,
+                stop=False,
+            )
+        for h in range(HALVES):
+            nc.tensor.matmul(banks[h][:], wt_sb[:, h * P : (h + 1) * P], tem[:], start=False, stop=True)
+
+        staged = [held.tile([P, N], F32, name=f"staged{h}") for h in range(HALVES)]
+        nc.vector.tensor_scalar_add(staged[0][:], banks[0][:], bias[0][:])
+        nc.scalar.activation(staged[1][:], banks[1][:], IDENTITY, bias=bias[1][:])
+        nc.sync.dma_start(out[0:P, :], staged[0][:])
+        nc.scalar.dma_start(out[P : 2 * P, :], staged[1][:])

@@ -20,23 +20,22 @@ def tile_xfmrnhpfast_kernel(tc, table, w, wt, b, t, freq, phase, offs, out):
     ):
         offsets = held.tile([P, N // 16], U16, name="offsets")
         nc.sync.dma_start(offsets[:], offs)
-        window = held.tile([P, S], BF16, name="window")
-        nc.sync.dma_start(window[:], table)
         w_sb = held.tile([P, HALVES * P], BF16, name="w_sb")
         nc.sync.dma_start(w_sb[:], w)
+        window = held.tile([P, S], BF16, name="window")
+        nc.sync.dma_start(window[:], table)
+        bias = [held.tile([P, 1], F32, name=f"bias{h}") for h in range(HALVES)]
+        for h in range(HALVES):
+            nc.sync.dma_start(bias[h][:], b[h * P : (h + 1) * P, :])
 
-        t_all = held.tile([P, N], F32, name="t_all")
-        nc.scalar.dma_start(t_all[:], t.to_broadcast([P, N]))
         freq_sb = held.tile([P, 1], F32, name="freq_sb")
         nc.scalar.dma_start(freq_sb[:], freq)
         phase_sb = held.tile([P, 1], F32, name="phase_sb")
         nc.scalar.dma_start(phase_sb[:], phase)
-
+        t_all = held.tile([P, N], F32, name="t_all")
+        nc.scalar.dma_start(t_all[:], t.to_broadcast([P, N]))
         wt_sb = held.tile([P, HALVES * P], BF16, name="wt_sb")
-        nc.gpsimd.dma_start(wt_sb[:], wt)
-        bias = [held.tile([P, 1], F32, name=f"bias{h}") for h in range(HALVES)]
-        for h in range(HALVES):
-            nc.gpsimd.dma_start(bias[h][:], b[h * P : (h + 1) * P, :])
+        nc.scalar.dma_start(wt_sb[:], wt)
 
         tem = held.tile([P, N], BF16, name="tem")
         nc.scalar.activation(tem[:], t_all[:], SIN, bias=phase_sb[:], scale=freq_sb[:])

@@ -18,24 +18,29 @@ def tile_xfmrnhpfast_kernel(tc, table, w, wt, b, t, freq, phase, offs, out):
         tc.tile_pool(name="held", bufs=1) as held,
         tc.psum_pool(name="psum", bufs=1) as psum,
     ):
+        scratch = held.tile([P, 1], F32, name="scratch")
+        nc.vector.memset(scratch[:], 0.0)
+        nc.scalar.activation(scratch[:], scratch[:], SIN)
+
         offsets = held.tile([P, N // 16], U16, name="offsets")
         nc.sync.dma_start(offsets[:], offs)
-        w_sb = held.tile([P, HALVES * P], BF16, name="w_sb")
-        nc.sync.dma_start(w_sb[:], w)
         window = held.tile([P, S], BF16, name="window")
         nc.sync.dma_start(window[:], table)
-        bias = [held.tile([P, 1], F32, name=f"bias{h}") for h in range(HALVES)]
-        for h in range(HALVES):
-            nc.sync.dma_start(bias[h][:], b[h * P : (h + 1) * P, :])
+        w_sb = held.tile([P, HALVES * P], BF16, name="w_sb")
+        nc.sync.dma_start(w_sb[:], w)
 
+        t_all = held.tile([P, N], F32, name="t_all")
+        nc.scalar.dma_start(t_all[:], t.to_broadcast([P, N]))
         freq_sb = held.tile([P, 1], F32, name="freq_sb")
         nc.scalar.dma_start(freq_sb[:], freq)
         phase_sb = held.tile([P, 1], F32, name="phase_sb")
         nc.scalar.dma_start(phase_sb[:], phase)
-        t_all = held.tile([P, N], F32, name="t_all")
-        nc.scalar.dma_start(t_all[:], t.to_broadcast([P, N]))
+
         wt_sb = held.tile([P, HALVES * P], BF16, name="wt_sb")
-        nc.scalar.dma_start(wt_sb[:], wt)
+        nc.gpsimd.dma_start(wt_sb[:], wt)
+        bias = [held.tile([P, 1], F32, name=f"bias{h}") for h in range(HALVES)]
+        for h in range(HALVES):
+            nc.gpsimd.dma_start(bias[h][:], b[h * P : (h + 1) * P, :])
 
         tem = held.tile([P, N], BF16, name="tem")
         nc.scalar.activation(tem[:], t_all[:], SIN, bias=phase_sb[:], scale=freq_sb[:])

@@ -8,6 +8,7 @@ P = 128
 S = 1024
 N = 512
 HALVES = 2
+WARM_MATMULS = 8
 
 FLOPS = 2 * (P + P) * (HALVES * P) * N
 
@@ -21,6 +22,12 @@ def tile_xfmrnhpfast_kernel(tc, table, w, wt, b, t, freq, phase, offs, out):
         scratch = held.tile([P, 1], F32, name="scratch")
         nc.vector.memset(scratch[:], 0.0)
         nc.scalar.activation(scratch[:], scratch[:], SIN)
+
+        zeros = held.tile([P, N], BF16, name="zeros")
+        nc.vector.memset(zeros[:], 0.0)
+        unused_bank = psum.tile([P, N], F32, name="unused_bank")
+        for i in range(WARM_MATMULS):
+            nc.tensor.matmul(unused_bank[:], zeros[:, 0:P], zeros[:], start=True, stop=True)
 
         offsets = held.tile([P, N // 16], U16, name="offsets")
         nc.sync.dma_start(offsets[:], offs)

@@ -9,6 +9,7 @@ S = 1024
 N = 512
 HALVES = 2
 WARM_MATMULS = 8
+PIECES = 2
 
 FLOPS = 2 * (P + P) * (HALVES * P) * N
 
@@ -65,7 +66,11 @@ def tile_xfmrnhpfast_kernel(tc, table, w, wt, b, t, freq, phase, offs, out):
             nc.tensor.matmul(banks[h][:], wt_sb[:, h * P : (h + 1) * P], tem[:], start=False, stop=True)
 
         staged = [held.tile([P, N], F32, name=f"staged{h}") for h in range(HALVES)]
-        nc.vector.tensor_scalar_add(staged[0][:], banks[0][:], bias[0][:])
-        nc.scalar.activation(staged[1][:], banks[1][:], IDENTITY, bias=bias[1][:])
-        nc.sync.dma_start(out[0:P, :], staged[0][:])
-        nc.scalar.dma_start(out[P : 2 * P, :], staged[1][:])
+        width = N // PIECES
+        for c in range(PIECES):
+            cols = slice(c * width, (c + 1) * width)
+            nc.vector.tensor_scalar_add(staged[0][:, cols], banks[0][:, cols], bias[0][:])
+            nc.sync.dma_start(out[0:P, cols], staged[0][:, cols])
+            nc.scalar.activation(staged[1][:, cols], banks[1][:, cols], IDENTITY, bias=bias[1][:])
+            values_queue = nc.scalar if c == PIECES - 1 else nc.sync
+            values_queue.dma_start(out[P : 2 * P, cols], staged[1][:, cols])

@@ -8,8 +8,10 @@ P = 128
 S = 1024
 N = 512
 HALVES = 2
-WARM_MATMULS = 8
 PIECES = 2
+WIDTH = N // PIECES
+LISTED = WIDTH // 16
+WARM_MATMULS = 8
 
 FLOPS = 2 * (P + P) * (HALVES * P) * N
 
@@ -30,6 +32,8 @@ def tile_xfmrnhpfast_kernel(tc, table, w, wt, b, t, freq, phase, offs, out):
         for i in range(WARM_MATMULS):
             nc.tensor.matmul(unused_bank[:], zeros[:, 0:P], zeros[:], start=True, stop=True)
 
+        t_all = held.tile([P, N], F32, name="t_all")
+        nc.sync.dma_start(t_all[:], t.to_broadcast([P, N]))
         offsets = held.tile([P, N // 16], U16, name="offsets")
         nc.sync.dma_start(offsets[:], offs)
         window = held.tile([P, S], BF16, name="window")
@@ -37,8 +41,6 @@ def tile_xfmrnhpfast_kernel(tc, table, w, wt, b, t, freq, phase, offs, out):
         w_sb = held.tile([P, HALVES * P], BF16, name="w_sb")
         nc.sync.dma_start(w_sb[:], w)
 
-        t_all = held.tile([P, N], F32, name="t_all")
-        nc.scalar.dma_start(t_all[:], t.to_broadcast([P, N]))
         freq_sb = held.tile([P, 1], F32, name="freq_sb")
         nc.scalar.dma_start(freq_sb[:], freq)
         phase_sb = held.tile([P, 1], F32, name="phase_sb")
@@ -50,27 +52,33 @@ def tile_xfmrnhpfast_kernel(tc, table, w, wt, b, t, freq, phase, offs, out):
         for h in range(HALVES):
             nc.gpsimd.dma_start(bias[h][:], b[h * P : (h + 1) * P, :])
 
-        tem = held.tile([P, N], BF16, name="tem")
-        nc.scalar.activation(tem[:], t_all[:], SIN, bias=phase_sb[:], scale=freq_sb[:])
-
-        banks = [psum.tile([P, N], F32, name=f"bank{h}") for h in range(HALVES)]
-        for h in range(HALVES):
-            nc.tensor.matmul(
-                banks[h][:],
-                w_sb[:, h * P : (h + 1) * P],
-                window[:].indirect(offsets[:]),
-                start=True,
-                stop=False,
+        tem = [held.tile([P, WIDTH], BF16, name=f"tem{c}") for c in range(PIECES)]
+        for c in range(PIECES):
+            nc.scalar.activation(
+                tem[c][:], t_all[:, c * WIDTH : (c + 1) * WIDTH], SIN, bias=phase_sb[:], scale=freq_sb[:]
             )
-        for h in range(HALVES):
-            nc.tensor.matmul(banks[h][:], wt_sb[:, h * P : (h + 1) * P], tem[:], start=False, stop=True)
+
+        banks = [[psum.tile([P, WIDTH], F32, name=f"bank{c}{h}") for h in range(HALVES)] for c in range(PIECES)]
+        for c in range(PIECES):
+            for h in range(HALVES):
+                nc.tensor.matmul(
+                    banks[c][h][:], wt_sb[:, h * P : (h + 1) * P], tem[c][:], start=True, stop=False
+                )
+        for c in range(PIECES):
+            for h in range(HALVES):
+                nc.tensor.matmul(
+                    banks[c][h][:],
+                    w_sb[:, h * P : (h + 1) * P],
+                    window[:].indirect(offsets[:, c * LISTED : (c + 1) * LISTED]),
+                    start=False,
+                    stop=True,
+                )
 
         staged = [held.tile([P, N], F32, name=f"staged{h}") for h in range(HALVES)]
-        width = N // PIECES
         for c in range(PIECES):
-            cols = slice(c * width, (c + 1) * width)
-            nc.vector.tensor_scalar_add(staged[0][:, cols], banks[0][:, cols], bias[0][:])
+            cols = slice(c * WIDTH, (c + 1) * WIDTH)
+            nc.vector.tensor_scalar_add(staged[0][:, cols], banks[c][0][:], bias[0][:])
             nc.sync.dma_start(out[0:P, cols], staged[0][:, cols])
-            nc.scalar.activation(staged[1][:, cols], banks[1][:, cols], IDENTITY, bias=bias[1][:])
+            nc.scalar.activation(staged[1][:, cols], banks[c][1][:], IDENTITY, bias=bias[1][:])
             values_queue = nc.scalar if c == PIECES - 1 else nc.sync
             values_queue.dma_start(out[P : 2 * P, cols], staged[1][:, cols])

@@ -11,7 +11,8 @@ HALVES = 2
 PIECES = 2
 WIDTH = N // PIECES
 LISTED = WIDTH // 16
-WARM_MATMULS = 8
+ROWS = 32
+WARM_MATMULS = 4
 
 FLOPS = 2 * (P + P) * (HALVES * P) * N
 
@@ -22,6 +23,9 @@ def tile_xfmrnhpfast_kernel(tc, table, w, wt, b, t, freq, phase, offs, out):
         tc.tile_pool(name="held", bufs=1) as held,
         tc.psum_pool(name="psum", bufs=1) as psum,
     ):
+        freq_rows = held.tile([ROWS, P], F32, name="freq_rows")
+        nc.vector.memset(freq_rows[:], 0.0)
+
         scratch = held.tile([P, 1], F32, name="scratch")
         nc.vector.memset(scratch[:], 0.0)
         nc.scalar.activation(scratch[:], scratch[:], SIN)
@@ -32,8 +36,12 @@ def tile_xfmrnhpfast_kernel(tc, table, w, wt, b, t, freq, phase, offs, out):
         for i in range(WARM_MATMULS):
             nc.tensor.matmul(unused_bank[:], zeros[:, 0:P], zeros[:], start=True, stop=True)
 
-        t_all = held.tile([P, N], F32, name="t_all")
-        nc.sync.dma_start(t_all[:], t.to_broadcast([P, N]))
+        t_rows = held.tile([ROWS, N], F32, name="t_rows")
+        nc.scalar.dma_start(t_rows[:], t.to_broadcast([ROWS, N]))
+        nc.scalar.dma_start(freq_rows[0:1, :], freq.rearrange("e o -> o e"))
+        phase_sb = held.tile([P, 1], F32, name="phase_sb")
+        nc.scalar.dma_start(phase_sb[:], phase)
+
         offsets = held.tile([P, N // 16], U16, name="offsets")
         nc.sync.dma_start(offsets[:], offs)
         window = held.tile([P, S], BF16, name="window")
@@ -41,28 +49,25 @@ def tile_xfmrnhpfast_kernel(tc, table, w, wt, b, t, freq, phase, offs, out):
         w_sb = held.tile([P, HALVES * P], BF16, name="w_sb")
         nc.sync.dma_start(w_sb[:], w)
 
-        freq_sb = held.tile([P, 1], F32, name="freq_sb")
-        nc.scalar.dma_start(freq_sb[:], freq)
-        phase_sb = held.tile([P, 1], F32, name="phase_sb")
-        nc.scalar.dma_start(phase_sb[:], phase)
-
         wt_sb = held.tile([P, HALVES * P], BF16, name="wt_sb")
         nc.gpsimd.dma_start(wt_sb[:], wt)
-        bias = [held.tile([P, 1], F32, name=f"bias{h}") for h in range(HALVES)]
-        for h in range(HALVES):
-            nc.gpsimd.dma_start(bias[h][:], b[h * P : (h + 1) * P, :])
+        bias = held.tile([P, HALVES], F32, name="bias")
+        nc.gpsimd.dma_start(bias[:], b.rearrange("(h p) o -> p (h o)", p=P))
 
-        tem = [held.tile([P, WIDTH], BF16, name=f"tem{c}") for c in range(PIECES)]
-        for c in range(PIECES):
-            nc.scalar.activation(
-                tem[c][:], t_all[:, c * WIDTH : (c + 1) * WIDTH], SIN, bias=phase_sb[:], scale=freq_sb[:]
-            )
+        product = psum.tile([P, N], F32, name="product")
+        nc.tensor.matmul(product[:], freq_rows[:], t_rows[:], start=True, stop=True)
+        tem = held.tile([P, N], BF16, name="tem")
+        nc.scalar.activation(tem[:], product[:], SIN, bias=phase_sb[:])
 
         banks = [[psum.tile([P, WIDTH], F32, name=f"bank{c}{h}") for h in range(HALVES)] for c in range(PIECES)]
         for c in range(PIECES):
             for h in range(HALVES):
                 nc.tensor.matmul(
-                    banks[c][h][:], wt_sb[:, h * P : (h + 1) * P], tem[c][:], start=True, stop=False
+                    banks[c][h][:],
+                    wt_sb[:, h * P : (h + 1) * P],
+                    tem[:, c * WIDTH : (c + 1) * WIDTH],
+                    start=True,
+                    stop=False,
                 )
         for c in range(PIECES):
             for h in range(HALVES):
@@ -77,8 +82,8 @@ def tile_xfmrnhpfast_kernel(tc, table, w, wt, b, t, freq, phase, offs, out):
         staged = [held.tile([P, N], F32, name=f"staged{h}") for h in range(HALVES)]
         for c in range(PIECES):
             cols = slice(c * WIDTH, (c + 1) * WIDTH)
-            nc.vector.tensor_scalar_add(staged[0][:, cols], banks[c][0][:], bias[0][:])
+            nc.vector.tensor_scalar_add(staged[0][:, cols], banks[c][0][:], bias[:, 0:1])
             nc.sync.dma_start(out[0:P, cols], staged[0][:, cols])
-            nc.scalar.activation(staged[1][:, cols], banks[c][1][:], IDENTITY, bias=bias[1][:])
+            nc.scalar.activation(staged[1][:, cols], banks[c][1][:], IDENTITY, bias=bias[:, 1:2])
             values_queue = nc.scalar if c == PIECES - 1 else nc.sync
             values_queue.dma_start(out[P : 2 * P, cols], staged[1][:, cols])

@@ -64,8 +64,8 @@ def tile_xfmrnhpfast_kernel(tc, table, w, wt, b, t, freq, phase, offs, out):
             for h in range(HALVES):
                 nc.tensor.matmul(
                     banks[c][h][:],
-                    wt_sb[:, h * P : (h + 1) * P],
-                    tem[:, c * WIDTH : (c + 1) * WIDTH],
+                    w_sb[:, h * P : (h + 1) * P],
+                    window[:].indirect(offsets[:, c * LISTED : (c + 1) * LISTED]),
                     start=True,
                     stop=False,
                 )
@@ -73,8 +73,8 @@ def tile_xfmrnhpfast_kernel(tc, table, w, wt, b, t, freq, phase, offs, out):
             for h in range(HALVES):
                 nc.tensor.matmul(
                     banks[c][h][:],
-                    w_sb[:, h * P : (h + 1) * P],
-                    window[:].indirect(offsets[:, c * LISTED : (c + 1) * LISTED]),
+                    wt_sb[:, h * P : (h + 1) * P],
+                    tem[:, c * WIDTH : (c + 1) * WIDTH],
                     start=False,
                     stop=True,
                 )

@@ -24,7 +24,7 @@ def tile_xfmrnhpfast_kernel(tc, table, w, wt, b, t, freq, phase, offs, out):
         tc.psum_pool(name="psum", bufs=1) as psum,
     ):
         freq_rows = held.tile([ROWS, P], F32, name="freq_rows")
-        nc.vector.memset(freq_rows[:], 0.0)
+        nc.gpsimd.memset(freq_rows[:], 0.0)
 
         scratch = held.tile([P, 1], F32, name="scratch")
         nc.vector.memset(scratch[:], 0.0)
@@ -36,12 +36,12 @@ def tile_xfmrnhpfast_kernel(tc, table, w, wt, b, t, freq, phase, offs, out):
         for i in range(WARM_MATMULS):
             nc.tensor.matmul(unused_bank[:], zeros[:, 0:P], zeros[:], start=True, stop=True)
 
-        t_rows = held.tile([ROWS, N], F32, name="t_rows")
-        nc.scalar.dma_start(t_rows[:], t.to_broadcast([ROWS, N]))
-        nc.scalar.dma_start(freq_rows[0:1, :], freq.rearrange("e o -> o e"))
         phase_sb = held.tile([P, 1], F32, name="phase_sb")
         nc.scalar.dma_start(phase_sb[:], phase)
 
+        t_rows = held.tile([ROWS, N], F32, name="t_rows")
+        nc.sync.dma_start(t_rows[:], t.to_broadcast([ROWS, N]))
+        nc.sync.dma_start(freq_rows[0:1, :], freq.rearrange("e o -> o e"))
         offsets = held.tile([P, N // 16], U16, name="offsets")
         nc.sync.dma_start(offsets[:], offs)
         window = held.tile([P, S], BF16, name="window")

@@ -11,8 +11,8 @@ HALVES = 2
 PIECES = 2
 WIDTH = N // PIECES
 LISTED = WIDTH // 16
-ROWS = 32
-WARM_MATMULS = 4
+PHASE_ROW = 1
+WARM_MATMULS = 14
 
 FLOPS = 2 * (P + P) * (HALVES * P) * N
 
@@ -23,41 +23,41 @@ def tile_xfmrnhpfast_kernel(tc, table, w, wt, b, t, freq, phase, offs, out):
         tc.tile_pool(name="held", bufs=1) as held,
         tc.psum_pool(name="psum", bufs=1) as psum,
     ):
-        freq_rows = held.tile([ROWS, P], F32, name="freq_rows")
-        nc.gpsimd.memset(freq_rows[:], 0.0)
+        freq_phase = held.tile([P, P], F32, name="freq_phase")
+        nc.gpsimd.memset(freq_phase[:], 0.0)
+        t_ones = held.tile([P, N], F32, name="t_ones")
+        nc.vector.memset(t_ones[:, 0 : N // 2], 1.0)
+        nc.gpsimd.memset(t_ones[:, N // 2 : N], 1.0)
 
         scratch = held.tile([P, 1], F32, name="scratch")
         nc.vector.memset(scratch[:], 0.0)
         nc.scalar.activation(scratch[:], scratch[:], SIN)
 
-        zeros = held.tile([P, N], BF16, name="zeros")
+        zeros = held.tile([P, P], BF16, name="zeros")
         nc.vector.memset(zeros[:], 0.0)
-        unused_bank = psum.tile([P, N], F32, name="unused_bank")
+        unused_bank = psum.tile([P, P], F32, name="unused_bank")
         for i in range(WARM_MATMULS):
-            nc.tensor.matmul(unused_bank[:], zeros[:, 0:P], zeros[:], start=True, stop=True)
+            nc.tensor.matmul(unused_bank[:], zeros[:], zeros[:], start=True, stop=True)
 
-        phase_sb = held.tile([P, 1], F32, name="phase_sb")
-        nc.scalar.dma_start(phase_sb[:], phase)
-
-        t_rows = held.tile([ROWS, N], F32, name="t_rows")
-        nc.sync.dma_start(t_rows[:], t.to_broadcast([ROWS, N]))
-        nc.sync.dma_start(freq_rows[0:1, :], freq.rearrange("e o -> o e"))
-        offsets = held.tile([P, N // 16], U16, name="offsets")
-        nc.sync.dma_start(offsets[:], offs)
         window = held.tile([P, S], BF16, name="window")
         nc.sync.dma_start(window[:], table)
+        nc.sync.dma_start(freq_phase[0:1, :], freq.rearrange("e o -> o e"))
+        nc.sync.dma_start(freq_phase[PHASE_ROW : PHASE_ROW + 1, :], phase.rearrange("e o -> o e"))
+        nc.sync.dma_start(t_ones[0:1, :], t)
         w_sb = held.tile([P, HALVES * P], BF16, name="w_sb")
         nc.sync.dma_start(w_sb[:], w)
+        offsets = held.tile([P, N // 16], U16, name="offsets")
+        nc.sync.dma_start(offsets[:], offs)
 
         wt_sb = held.tile([P, HALVES * P], BF16, name="wt_sb")
         nc.gpsimd.dma_start(wt_sb[:], wt)
         bias = held.tile([P, HALVES], F32, name="bias")
         nc.gpsimd.dma_start(bias[:], b.rearrange("(h p) o -> p (h o)", p=P))
 
-        product = psum.tile([P, N], F32, name="product")
-        nc.tensor.matmul(product[:], freq_rows[:], t_rows[:], start=True, stop=True)
+        argument = psum.tile([P, N], F32, name="argument")
+        nc.tensor.matmul(argument[:], freq_phase[:], t_ones[:], start=True, stop=True)
         tem = held.tile([P, N], BF16, name="tem")
-        nc.scalar.activation(tem[:], product[:], SIN, bias=phase_sb[:])
+        nc.scalar.activation(tem[:], argument[:], SIN)
 
         banks = [[psum.tile([P, WIDTH], F32, name=f"bank{c}{h}") for h in range(HALVES)] for c in range(PIECES)]
         for c in range(PIECES):

@@ -1,4 +1,5 @@
 import concourse.mybir as mybir
+from concourse.masks import make_identity
 
 BF16, F32, U16 = mybir.dt.bfloat16, mybir.dt.float32, mybir.dt.uint16
 SIN = mybir.ActivationFunctionType.Sin
@@ -11,8 +12,8 @@ HALVES = 2
 PIECES = 2
 WIDTH = N // PIECES
 LISTED = WIDTH // 16
-PHASE_ROW = 1
-WARM_MATMULS = 14
+BLOCKS = N // P
+WARM_MATMULS = 16
 
 FLOPS = 2 * (P + P) * (HALVES * P) * N
 
@@ -23,41 +24,46 @@ def tile_xfmrnhpfast_kernel(tc, table, w, wt, b, t, freq, phase, offs, out):
         tc.tile_pool(name="held", bufs=1) as held,
         tc.psum_pool(name="psum", bufs=1) as psum,
     ):
-        freq_phase = held.tile([P, P], F32, name="freq_phase")
-        nc.gpsimd.memset(freq_phase[:], 0.0)
-        t_ones = held.tile([P, N], F32, name="t_ones")
-        nc.vector.memset(t_ones[:, 0 : N // 2], 1.0)
-        nc.gpsimd.memset(t_ones[:, N // 2 : N], 1.0)
-
-        scratch = held.tile([P, 1], F32, name="scratch")
-        nc.vector.memset(scratch[:], 0.0)
-        nc.scalar.activation(scratch[:], scratch[:], SIN)
-
         zeros = held.tile([P, P], BF16, name="zeros")
         nc.vector.memset(zeros[:], 0.0)
         unused_bank = psum.tile([P, P], F32, name="unused_bank")
         for i in range(WARM_MATMULS):
             nc.tensor.matmul(unused_bank[:], zeros[:], zeros[:], start=True, stop=True)
 
+        scratch = held.tile([P, 1], F32, name="scratch")
+        nc.vector.memset(scratch[:], 0.0)
+        nc.scalar.activation(scratch[:], scratch[:], SIN)
+
+        t_columns = held.tile([P, BLOCKS], F32, name="t_columns")
+        nc.scalar.dma_start(t_columns[:], t.rearrange("o (c p) -> p (o c)", p=P))
+        freq_sb = held.tile([P, 1], F32, name="freq_sb")
+        nc.scalar.dma_start(freq_sb[:], freq)
+        phase_sb = held.tile([P, 1], F32, name="phase_sb")
+        nc.scalar.dma_start(phase_sb[:], phase)
+
+        bias = held.tile([P, HALVES], F32, name="bias")
+        nc.scalar.dma_start(bias[:], b.rearrange("(h p) o -> p (h o)", p=P))
+
         window = held.tile([P, S], BF16, name="window")
         nc.sync.dma_start(window[:], table)
-        nc.sync.dma_start(freq_phase[0:1, :], freq.rearrange("e o -> o e"))
-        nc.sync.dma_start(freq_phase[PHASE_ROW : PHASE_ROW + 1, :], phase.rearrange("e o -> o e"))
-        nc.sync.dma_start(t_ones[0:1, :], t)
         w_sb = held.tile([P, HALVES * P], BF16, name="w_sb")
         nc.sync.dma_start(w_sb[:], w)
+        wt_sb = held.tile([P, HALVES * P], BF16, name="wt_sb")
+        nc.sync.dma_start(wt_sb[:], wt)
         offsets = held.tile([P, N // 16], U16, name="offsets")
         nc.sync.dma_start(offsets[:], offs)
 
-        wt_sb = held.tile([P, HALVES * P], BF16, name="wt_sb")
-        nc.gpsimd.dma_start(wt_sb[:], wt)
-        bias = held.tile([P, HALVES], F32, name="bias")
-        nc.gpsimd.dma_start(bias[:], b.rearrange("(h p) o -> p (h o)", p=P))
+        identity = held.tile([P, P], F32, name="identity")
+        make_identity(nc, identity[:])
 
-        argument = psum.tile([P, N], F32, name="argument")
-        nc.tensor.matmul(argument[:], freq_phase[:], t_ones[:], start=True, stop=True)
+        t_all = psum.tile([P, N], F32, name="t_all")
+        for c in range(BLOCKS):
+            nc.tensor.transpose(
+                t_all[:, c * P : (c + 1) * P], t_columns[:, c : c + 1].to_broadcast([P, P]), identity[:]
+            )
+
         tem = held.tile([P, N], BF16, name="tem")
-        nc.scalar.activation(tem[:], argument[:], SIN)
+        nc.scalar.activation(tem[:], t_all[:], SIN, bias=phase_sb[:], scale=freq_sb[:])
 
         banks = [[psum.tile([P, WIDTH], F32, name=f"bank{c}{h}") for h in range(HALVES)] for c in range(PIECES)]
         for c in range(PIECES):

@@ -13,7 +13,7 @@ PIECES = 2
 WIDTH = N // PIECES
 LISTED = WIDTH // 16
 BLOCKS = N // P
-WARM_MATMULS = 16
+WARM_MATMULS = 12
 
 FLOPS = 2 * (P + P) * (HALVES * P) * N
 
@@ -35,23 +35,22 @@ def tile_xfmrnhpfast_kernel(tc, table, w, wt, b, t, freq, phase, offs, out):
         nc.scalar.activation(scratch[:], scratch[:], SIN)
 
         t_columns = held.tile([P, BLOCKS], F32, name="t_columns")
-        nc.scalar.dma_start(t_columns[:], t.rearrange("o (c p) -> p (o c)", p=P))
+        nc.sync.dma_start(t_columns[:], t.rearrange("o (c p) -> p (o c)", p=P))
         freq_sb = held.tile([P, 1], F32, name="freq_sb")
-        nc.scalar.dma_start(freq_sb[:], freq)
+        nc.sync.dma_start(freq_sb[:], freq)
         phase_sb = held.tile([P, 1], F32, name="phase_sb")
-        nc.scalar.dma_start(phase_sb[:], phase)
-
-        bias = held.tile([P, HALVES], F32, name="bias")
-        nc.scalar.dma_start(bias[:], b.rearrange("(h p) o -> p (h o)", p=P))
-
+        nc.sync.dma_start(phase_sb[:], phase)
+        wt_sb = held.tile([P, HALVES * P], BF16, name="wt_sb")
+        nc.sync.dma_start(wt_sb[:], wt)
         window = held.tile([P, S], BF16, name="window")
         nc.sync.dma_start(window[:], table)
         w_sb = held.tile([P, HALVES * P], BF16, name="w_sb")
         nc.sync.dma_start(w_sb[:], w)
-        wt_sb = held.tile([P, HALVES * P], BF16, name="wt_sb")
-        nc.sync.dma_start(wt_sb[:], wt)
         offsets = held.tile([P, N // 16], U16, name="offsets")
         nc.sync.dma_start(offsets[:], offs)
+
+        bias = held.tile([P, HALVES], F32, name="bias")
+        nc.scalar.dma_start(bias[:], b.rearrange("(h p) o -> p (h o)", p=P))
 
         identity = held.tile([P, P], F32, name="identity")
         make_identity(nc, identity[:])
@@ -70,8 +69,8 @@ def tile_xfmrnhpfast_kernel(tc, table, w, wt, b, t, freq, phase, offs, out):
             for h in range(HALVES):
                 nc.tensor.matmul(
                     banks[c][h][:],
-                    w_sb[:, h * P : (h + 1) * P],
-                    window[:].indirect(offsets[:, c * LISTED : (c + 1) * LISTED]),
+                    wt_sb[:, h * P : (h + 1) * P],
+                    tem[:, c * WIDTH : (c + 1) * WIDTH],
                     start=True,
                     stop=False,
                 )
@@ -79,8 +78,8 @@ def tile_xfmrnhpfast_kernel(tc, table, w, wt, b, t, freq, phase, offs, out):
             for h in range(HALVES):
                 nc.tensor.matmul(
                     banks[c][h][:],
-                    wt_sb[:, h * P : (h + 1) * P],
-                    tem[:, c * WIDTH : (c + 1) * WIDTH],
+                    w_sb[:, h * P : (h + 1) * P],
+                    window[:].indirect(offsets[:, c * LISTED : (c + 1) * LISTED]),
                     start=False,
                     stop=True,
                 )

import concourse.mybir as mybir
from concourse.masks import make_identity

BF16, F32, U16 = mybir.dt.bfloat16, mybir.dt.float32, mybir.dt.uint16
SIN = mybir.ActivationFunctionType.Sin
IDENTITY = mybir.ActivationFunctionType.Identity

P = 128
S = 1024
N = 512
HALVES = 2
PIECES = 2
WIDTH = N // PIECES
LISTED = WIDTH // 16
BLOCKS = N // P
WARM_MATMULS = 12

FLOPS = 2 * (P + P) * (HALVES * P) * N


def tile_xfmrnhpfast_kernel(tc, table, w, wt, b, t, freq, phase, offs, out):
    nc = tc.nc
    with (
        tc.tile_pool(name="held", bufs=1) as held,
        tc.psum_pool(name="psum", bufs=1) as psum,
    ):
        zeros = held.tile([P, P], BF16, name="zeros")
        nc.vector.memset(zeros[:], 0.0)
        unused_bank = psum.tile([P, P], F32, name="unused_bank")
        for i in range(WARM_MATMULS):
            nc.tensor.matmul(unused_bank[:], zeros[:], zeros[:], start=True, stop=True)

        scratch = held.tile([P, 1], F32, name="scratch")
        nc.vector.memset(scratch[:], 0.0)
        nc.scalar.activation(scratch[:], scratch[:], SIN)

        t_columns = held.tile([P, BLOCKS], F32, name="t_columns")
        nc.sync.dma_start(t_columns[:], t.rearrange("o (c p) -> p (o c)", p=P))
        freq_sb = held.tile([P, 1], F32, name="freq_sb")
        nc.sync.dma_start(freq_sb[:], freq)
        phase_sb = held.tile([P, 1], F32, name="phase_sb")
        nc.sync.dma_start(phase_sb[:], phase)
        wt_sb = held.tile([P, HALVES * P], BF16, name="wt_sb")
        nc.sync.dma_start(wt_sb[:], wt)
        window = held.tile([P, S], BF16, name="window")
        nc.sync.dma_start(window[:], table)
        w_sb = held.tile([P, HALVES * P], BF16, name="w_sb")
        nc.sync.dma_start(w_sb[:], w)
        offsets = held.tile([P, N // 16], U16, name="offsets")
        nc.sync.dma_start(offsets[:], offs)

        bias = held.tile([P, HALVES], F32, name="bias")
        nc.scalar.dma_start(bias[:], b.rearrange("(h p) o -> p (h o)", p=P))

        identity = held.tile([P, P], F32, name="identity")
        make_identity(nc, identity[:])

        t_all = psum.tile([P, N], F32, name="t_all")
        for c in range(BLOCKS):
            nc.tensor.transpose(
                t_all[:, c * P : (c + 1) * P], t_columns[:, c : c + 1].to_broadcast([P, P]), identity[:]
            )

        tem = held.tile([P, N], BF16, name="tem")
        nc.scalar.activation(tem[:], t_all[:], SIN, bias=phase_sb[:], scale=freq_sb[:])

        banks = [[psum.tile([P, WIDTH], F32, name=f"bank{c}{h}") for h in range(HALVES)] for c in range(PIECES)]
        for c in range(PIECES):
            for h in range(HALVES):
                nc.tensor.matmul(
                    banks[c][h][:],
                    wt_sb[:, h * P : (h + 1) * P],
                    tem[:, c * WIDTH : (c + 1) * WIDTH],
                    start=True,
                    stop=False,
                )
        for c in range(PIECES):
            for h in range(HALVES):
                nc.tensor.matmul(
                    banks[c][h][:],
                    w_sb[:, h * P : (h + 1) * P],
                    window[:].indirect(offsets[:, c * LISTED : (c + 1) * LISTED]),
                    start=False,
                    stop=True,
                )

        staged = [held.tile([P, N], F32, name=f"staged{h}") for h in range(HALVES)]
        for c in range(PIECES):
            cols = slice(c * WIDTH, (c + 1) * WIDTH)
            nc.vector.tensor_scalar_add(staged[0][:, cols], banks[c][0][:], bias[:, 0:1])
            nc.sync.dma_start(out[0:P, cols], staged[0][:, cols])
            nc.scalar.activation(staged[1][:, cols], banks[c][1][:], IDENTITY, bias=bias[:, 1:2])
            values_queue = nc.scalar if c == PIECES - 1 else nc.sync
            values_queue.dma_start(out[P : 2 * P, cols], staged[1][:, cols])
